import numpy as np
import ml_dtypes


def mxq(x, axis, fmt="e4m3"):
    dtype, down = {"e4m3": (ml_dtypes.float8_e4m3fn, 7), "e5m2": (ml_dtypes.float8_e5m2, 14)}[fmt]
    v = np.moveaxis(np.asarray(x, np.float32).astype(ml_dtypes.bfloat16).astype(np.float64), axis, -1)
    blocks = v.reshape(v.shape[:-1] + (-1, 32))
    amax = np.abs(blocks).max(-1, keepdims=True)
    byte = np.maximum(np.where(amax > 0, np.frexp(amax)[1] - 1 + 127, 0) - down, 1)
    scale = np.exp2(byte - 127.0)
    codes = (blocks / scale).astype(np.float32).astype(dtype).astype(np.float64)
    return np.moveaxis((codes * scale).reshape(v.shape), -1, axis)


WIDE = False


def mx_kscale(k):
    if not WIDE:
        return np.ones(k)
    levels = np.array([10, -10, 5, -5, 0])
    a = np.random.permutation(np.resize(levels, k // 512 * 4)).reshape(k // 512, 4)
    idx = np.arange(k)
    return np.exp2(a[idx // 512, idx % 128 // 32])


BF16 = ml_dtypes.bfloat16


def bf(x):
    return np.asarray(x, np.float32).astype(BF16)


def f64(x):
    return np.asarray(x).astype(np.float64)


E2M1 = np.array([0.0, 0.5, 1.0, 1.5, 2.0, 3.0, 4.0, 6.0, -0.0, -0.5, -1.0, -1.5, -2.0, -3.0, -4.0, -6.0])


def pack_weight(w, fmt):
    k, n = w.shape
    w = f64(bf(w)).reshape(k // 32, 32, n)
    amax = np.abs(w).max(1)
    if fmt == "e4m3":
        byte = np.frexp(amax)[1] - 1 + 127 - 7
    else:
        mant, ex = np.frexp(amax / 6.0)
        byte = np.where(mant > 0.5, ex, ex - 1) + 127
    byte = np.clip(np.where(amax > 0, byte, 1), 1, 254)
    scaled = (w * np.exp2(127.0 - byte)[:, None, :]).reshape(k, n).astype(np.float32)
    by_word = np.ascontiguousarray(scaled.reshape(k // 512, 128, 4, n).transpose(0, 1, 3, 2))
    if fmt == "e4m3":
        words = by_word.astype(ml_dtypes.float8_e4m3fn).view(np.uint8)
    else:
        c = by_word.astype(ml_dtypes.float4_e2m1fn).view(np.uint8) & 0xF
        words = c[..., 0::2] | (c[..., 1::2] << 4)
    return np.ascontiguousarray(words), np.ascontiguousarray(byte.astype(np.uint8).reshape(k // 512, 16, n))


def unpack_weight(words, scales, fmt):
    g, p, n, _ = words.shape
    if fmt == "e4m3":
        vals = np.ascontiguousarray(words).view(ml_dtypes.float8_e4m3fn).astype(np.float64)
    else:
        nib = np.empty((g, p, n, 4), np.uint8)
        nib[..., 0::2] = words & 0xF
        nib[..., 1::2] = words >> 4
        vals = E2M1[nib]
    vals = vals * np.repeat(np.exp2(scales.astype(np.float64) - 127.0), 8, axis=1)[..., None]
    return vals.transpose(0, 1, 3, 2).reshape(g * 512, n)

def pack4(w):
    words, scales = pack_weight(w, "e2m1")
    return words.reshape(words.shape[0], 128, -1), scales


def unpack4(words, scales):
    return unpack_weight(words.reshape(words.shape[0], 128, -1, 2), scales, "e2m1")


B, S, D_MODEL, N_HEADS, QK_ROPE, QK_NOPE, KV_LORA, V_DIM = 2, 256, 2048, 16, 128, 128, 512, 128
QK_DIM = QK_ROPE + QK_NOPE
ROPE_BASE = 10000.0


def apply_rope(r):
    freqs = 1.0 / (ROPE_BASE ** (np.arange(0, QK_ROPE, 2) / QK_ROPE))
    t = np.arange(S)[:, None] * freqs[None, :]
    cos = np.cos(t)[None, :, None, :]
    sin = np.sin(t)[None, :, None, :]
    r1 = r[..., 0::2]
    r2 = r[..., 1::2]
    return np.stack([r1 * cos - r2 * sin, r2 * cos + r1 * sin], axis=-1).reshape(r.shape)


def setup_inputs():
    s = mx_kscale(D_MODEL)
    x = bf(np.random.standard_normal((B, S, D_MODEL)) * s)
    words, scales = pack4(np.random.standard_normal((D_MODEL, N_HEADS * QK_DIM)) / np.sqrt(D_MODEL) / s[:, None])
    return {"x": x, "Wq_words": words, "Wq_scales": scales}


def reference(x, Wq_words, Wq_scales):
    q = (mxq(f64(x), 2, "e4m3") @ unpack4(Wq_words, Wq_scales)).reshape(B, S, N_HEADS, QK_DIM)
    q_nope, q_rope = q[..., :QK_NOPE], q[..., QK_NOPE:]
    return np.concatenate([q_nope, apply_rope(q_rope)], axis=-1)

@@ -1,0 +1,251 @@
+import math
+from contextlib import ExitStack
+
+import concourse.mybir as mybir
+from concourse.masks import make_identity
+
+F32 = mybir.dt.float32
+BF16 = mybir.dt.bfloat16
+I32 = mybir.dt.int32
+U32 = mybir.dt.uint32
+U8 = mybir.dt.uint8
+FP8X4 = mybir.dt.float8_e4m3fn_x4
+FP4X4 = mybir.dt.float4_e2m1fn_x4
+ALU = mybir.AluOpType
+ACT = mybir.ActivationFunctionType
+
+P = 128
+TOKENS = 512
+SEQ = 256
+D_MODEL = 2048
+D_OUT = 4096
+HEAD = 256
+PAIRS = 64
+ROPE_BASE = 10000.0
+
+K_PASS = 4 * P
+PASSES = D_MODEL // K_PASS
+TOKEN_TILES = TOKENS // P
+BANK = 512
+BANK_HEADS = BANK // HEAD
+STRIPE = 2 * BANK
+STRIPES = D_OUT // STRIPE
+
+FLOPS = 2 * TOKENS * D_MODEL * D_OUT
+
+ROUND_MAGIC = 1.5 * 2.0**23
+PI_HI = 3.140625
+PI_MID = round((math.pi - PI_HI) * 2.0**22) / 2.0**22
+PI_LO = math.pi - PI_HI - PI_MID
+
+
+def build_rope_tables(nc, pool):
+    warm = pool.tile([P, 1], F32)
+    nc.vector.memset(warm[:], 0.0)
+    nc.scalar.activation(out=warm[:], in_=warm[:], func=ACT.Sin)
+
+    freq = pool.tile([P, PAIRS], F32)
+    nc.vector.memset(freq[:, 0:1], 1.0)
+    for done in (1, 2, 4, 8, 16, 32):
+        nc.vector.tensor_scalar(
+            out=freq[:, done : 2 * done],
+            in0=freq[:, 0:done],
+            scalar1=ROPE_BASE ** (-2.0 * done / (2 * PAIRS)),
+            scalar2=None,
+            op0=ALU.mult,
+        )
+
+    position_int = pool.tile([P, 2], I32)
+    nc.gpsimd.iota(position_int[:], pattern=[[P, 2]], base=0, channel_multiplier=1)
+    position = pool.tile([P, 2], F32)
+    nc.vector.tensor_copy(out=position[:], in_=position_int[:])
+
+    angle = pool.tile([P, 2, PAIRS], F32)
+    for half in range(2):
+        nc.vector.tensor_scalar(
+            out=angle[:, half, :],
+            in0=freq[:],
+            scalar1=position[:, half : half + 1],
+            scalar2=None,
+            op0=ALU.mult,
+        )
+
+    shifted = pool.tile([P, 2, PAIRS], F32)
+    nc.vector.tensor_scalar(
+        out=shifted[:],
+        in0=angle[:],
+        scalar1=1.0 / math.pi,
+        scalar2=ROUND_MAGIC,
+        op0=ALU.mult,
+        op1=ALU.add,
+    )
+    odd_n = pool.tile([P, 2, PAIRS], I32)
+    nc.vector.tensor_scalar(
+        out=odd_n[:], in0=shifted[:].bitcast(I32), scalar1=1, scalar2=None, op0=ALU.bitwise_and
+    )
+    sign = pool.tile([P, 2, PAIRS], F32)
+    nc.vector.tensor_scalar(
+        out=sign[:], in0=odd_n[:], scalar1=-2.0, scalar2=1.0, op0=ALU.mult, op1=ALU.add
+    )
+    n = pool.tile([P, 2, PAIRS], F32)
+    nc.vector.tensor_scalar(
+        out=n[:], in0=shifted[:], scalar1=ROUND_MAGIC, scalar2=None, op0=ALU.subtract
+    )
+    rest = pool.tile([P, 2, PAIRS], F32)
+    nc.vector.scalar_tensor_tensor(
+        out=rest[:], in0=n[:], scalar=-PI_HI, in1=angle[:], op0=ALU.mult, op1=ALU.add
+    )
+    for piece in (PI_MID, PI_LO):
+        nc.vector.scalar_tensor_tensor(
+            out=rest[:], in0=n[:], scalar=-piece, in1=rest[:], op0=ALU.mult, op1=ALU.add
+        )
+    rest_abs = pool.tile([P, 2, PAIRS], F32)
+    nc.vector.scalar_tensor_tensor(
+        out=rest_abs[:], in0=rest[:], scalar=-1.0, in1=rest[:], op0=ALU.mult, op1=ALU.max
+    )
+    sin_rest = pool.tile([P, 2, PAIRS], F32)
+    nc.scalar.activation(out=sin_rest[:], in_=rest[:], func=ACT.Sin)
+    cos_rest = pool.tile([P, 2, PAIRS], F32)
+    nc.scalar.activation(
+        out=cos_rest[:], in_=rest_abs[:], func=ACT.Sin, scale=-1.0, bias=math.pi / 2.0
+    )
+
+    by_even = pool.tile([P, 2, PAIRS, 2], F32)
+    by_odd = pool.tile([P, 2, PAIRS, 2], F32)
+    nc.vector.tensor_tensor(out=by_even[:, :, :, 0], in0=cos_rest[:], in1=sign[:], op=ALU.mult)
+    nc.vector.tensor_tensor(out=by_even[:, :, :, 1], in0=sin_rest[:], in1=sign[:], op=ALU.mult)
+    nc.vector.scalar_tensor_tensor(
+        out=by_odd[:, :, :, 0],
+        in0=sin_rest[:],
+        scalar=-1.0,
+        in1=sign[:],
+        op0=ALU.mult,
+        op1=ALU.mult,
+    )
+    nc.vector.tensor_tensor(out=by_odd[:, :, :, 1], in0=cos_rest[:], in1=sign[:], op=ALU.mult)
+    return by_even, by_odd
+
+
+def tile_multiheadlatentattention_pb_kernel(tc, x, Wq_words, Wq_scales, out):
+    nc = tc.nc
+    x_rows = x.flatten_outer_dims()
+    out_rows = out.rearrange("b s h d -> (b s) (h d)")
+    words_in = Wq_words.bitcast(I32).rearrange("g p n -> p g n")
+    scales_in = Wq_scales.bitcast(I32).rearrange("g q n -> q g n")
+
+    with ExitStack() as ctx:
+        keep = ctx.enter_context(tc.tile_pool(name="keep", bufs=1))
+        stage = ctx.enter_context(tc.tile_pool(name="stage", bufs=2))
+        work = ctx.enter_context(tc.tile_pool(name="work", bufs=4))
+        results = ctx.enter_context(tc.tile_pool(name="results", bufs=4))
+        psum_x = ctx.enter_context(tc.psum_pool(name="psum_x", bufs=2))
+        psum_q = ctx.enter_context(tc.psum_pool(name="psum_q", bufs=6))
+
+        x_sb = [keep.tile([P, D_MODEL], BF16, name="x_sb%d" % t) for t in range(TOKEN_TILES)]
+        x_codes = keep.tile([P, TOKEN_TILES, PASSES * P], U32, align_bytes=64)
+        x_scales = keep.tile([P, TOKEN_TILES, PASSES * P], U8, align_bytes=64)
+        w_words = keep.tile([P, PASSES, 2 * D_OUT], U8, align_bytes=64)
+        w_scales = keep.tile([P, PASSES, D_OUT], U8, align_bytes=64)
+
+        def load_x(t):
+            nc.sync.dma_start(out=x_sb[t][:], in_=x_rows[t * P : (t + 1) * P, :])
+
+        def load_weight_stripe(s):
+            nc.vector.memset(w_scales[:, :, s * STRIPE : (s + 1) * STRIPE].bitcast(I32), 0)
+            for q in range(8):
+                first = 32 * (q // 4) + q % 4
+                nc.sync.dma_start(
+                    out=w_scales[first:P:64, :, s * STRIPE : (s + 1) * STRIPE].bitcast(I32),
+                    in_=scales_in[q:16:8, :, s * STRIPE // 4 : (s + 1) * STRIPE // 4],
+                )
+            nc.sync.dma_start(
+                out=w_words[:, :, 2 * s * STRIPE : 2 * (s + 1) * STRIPE].bitcast(I32),
+                in_=words_in[:, :, s * STRIPE // 2 : (s + 1) * STRIPE // 2],
+            )
+
+        def quantise_x(t):
+            x_words = x_sb[t][:].bitcast(F32)
+            grouped = stage.tile([P, D_MODEL], BF16, align_bytes=64)
+            grouped_words = grouped[:].bitcast(F32).rearrange(
+                "p (g m u) -> p g m u", g=PASSES, u=2
+            )
+            for b in range(2):
+                flipped = psum_x.tile([P, 4, P], F32)
+                for j in range(4):
+                    g, u = 2 * b + j // 2, j % 2
+                    nc.tensor.transpose(
+                        flipped[:, j, :],
+                        x_words[:, 256 * g + u : 256 * (g + 1) : 2],
+                        identity[:],
+                    )
+                nc.scalar.copy(
+                    out=grouped_words[:, 2 * b : 2 * b + 2, :, :],
+                    in_=flipped[:].rearrange("p (g u) m -> p g m u", u=2),
+                )
+            nc.vector.quantize_mx(
+                out=x_codes[:, t, :].bitcast(FP8X4), scales=x_scales[:, t, :], in_=grouped[:]
+            )
+
+        def project(t, s):
+            half = t % (SEQ // P)
+            even_table = by_even[:, half, :, :].unsqueeze(1).to_broadcast([P, BANK_HEADS, PAIRS, 2])
+            odd_table = by_odd[:, half, :, :].unsqueeze(1).to_broadcast([P, BANK_HEADS, PAIRS, 2])
+            result = results.tile([P, STRIPE], F32)
+            for b in range(STRIPE // BANK):
+                c = s * STRIPE + b * BANK
+                acc = psum_q.tile([P, BANK], F32)
+                for g in range(PASSES):
+                    nc.tensor.matmul_mx(
+                        out=acc[:],
+                        lhsT=x_codes[:, t, g * P : (g + 1) * P].bitcast(FP8X4),
+                        lhsT_scale=x_scales[:, t, g * P : (g + 1) * P],
+                        rhs=w_words[:, g, 2 * c : 2 * (c + BANK)].bitcast(FP4X4),
+                        rhs_scale=w_scales[:, g, c : c + BANK],
+                        start=(g == 0),
+                        stop=(g == PASSES - 1),
+                    )
+                heads = acc[:].rearrange("p (h f i e) -> p h f i e", h=BANK_HEADS, f=2, e=2)
+                res = result[:, b * BANK : (b + 1) * BANK].rearrange(
+                    "p (h f i e) -> p h f i e", h=BANK_HEADS, f=2, e=2
+                )
+                nc.scalar.copy(out=res[:, :, 0, :, :], in_=heads[:, :, 0, :, :])
+                from_odd = work.tile([P, BANK_HEADS, PAIRS, 2], F32)
+                nc.vector.tensor_tensor(
+                    out=res[:, :, 1, :, :],
+                    in0=heads[:, :, 1, :, 0:1].to_broadcast([P, BANK_HEADS, PAIRS, 2]),
+                    in1=even_table,
+                    op=ALU.mult,
+                )
+                nc.vector.tensor_tensor(
+                    out=from_odd[:],
+                    in0=heads[:, :, 1, :, 1:2].to_broadcast([P, BANK_HEADS, PAIRS, 2]),
+                    in1=odd_table,
+                    op=ALU.mult,
+                )
+                nc.gpsimd.tensor_tensor(
+                    out=res[:, :, 1, :, :], in0=res[:, :, 1, :, :], in1=from_odd[:], op=ALU.add
+                )
+            nc.sync.dma_start(
+                out=out_rows[t * P : (t + 1) * P, s * STRIPE : (s + 1) * STRIPE], in_=result[:]
+            )
+
+        load_x(0)
+        load_weight_stripe(0)
+        for t in range(1, TOKEN_TILES):
+            load_x(t)
+
+        identity = keep.tile([P, P], F32)
+        make_identity(nc, identity[:])
+        by_even, by_odd = build_rope_tables(nc, keep)
+
+        quantise_x(0)
+        for s in range(1, STRIPES):
+            load_weight_stripe(s)
+
+        for t in range(TOKEN_TILES):
+            if t + 1 < TOKEN_TILES:
+                quantise_x(t + 1)
+            project(t, 0)
+        for s in range(1, STRIPES):
+            for t in range(TOKEN_TILES):
+                project(t, s)

@@ -28,7 +28,8 @@ PASSES = D_MODEL // K_PASS
 TOKEN_TILES = TOKENS // P
 BANK = 512
 BANK_HEADS = BANK // HEAD
-STRIPE = 2 * BANK
+STRIPE_BANKS = 2
+STRIPE = STRIPE_BANKS * BANK
 STRIPES = D_OUT // STRIPE
 
 FLOPS = 2 * TOKENS * D_MODEL * D_OUT
@@ -137,31 +138,43 @@ def tile_multiheadlatentattention_pb_kernel(tc, x, Wq_words, Wq_scales, out):
         keep = ctx.enter_context(tc.tile_pool(name="keep", bufs=1))
         stage = ctx.enter_context(tc.tile_pool(name="stage", bufs=2))
         work = ctx.enter_context(tc.tile_pool(name="work", bufs=4))
-        results = ctx.enter_context(tc.tile_pool(name="results", bufs=4))
+        results = ctx.enter_context(tc.tile_pool(name="results", bufs=12))
         psum_x = ctx.enter_context(tc.psum_pool(name="psum_x", bufs=2))
         psum_q = ctx.enter_context(tc.psum_pool(name="psum_q", bufs=6))
 
         x_sb = [keep.tile([P, D_MODEL], BF16, name="x_sb%d" % t) for t in range(TOKEN_TILES)]
-        x_codes = keep.tile([P, TOKEN_TILES, PASSES * P], U32, align_bytes=64)
-        x_scales = keep.tile([P, TOKEN_TILES, PASSES * P], U8, align_bytes=64)
-        w_words = keep.tile([P, PASSES, 2 * D_OUT], U8, align_bytes=64)
-        w_scales = keep.tile([P, PASSES, D_OUT], U8, align_bytes=64)
+        x_codes = [
+            keep.tile([P, PASSES * P], U32, name="x_codes%d" % t, align_bytes=64)
+            for t in range(TOKEN_TILES)
+        ]
+        x_scales = [
+            keep.tile([P, PASSES * P], U8, name="x_scales%d" % t, align_bytes=64)
+            for t in range(TOKEN_TILES)
+        ]
+        w_words = [
+            keep.tile([P, PASSES, 2 * BANK], U8, name="w_words%d" % c, align_bytes=64)
+            for c in range(D_OUT // BANK)
+        ]
+        w_scales = [
+            keep.tile([P, PASSES, STRIPE], U8, name="w_scales%d" % s, align_bytes=64)
+            for s in range(STRIPES)
+        ]
 
         def load_x(t):
             nc.sync.dma_start(out=x_sb[t][:], in_=x_rows[t * P : (t + 1) * P, :])
 
         def load_weight_stripe(s):
-            nc.vector.memset(w_scales[:, :, s * STRIPE : (s + 1) * STRIPE].bitcast(I32), 0)
-            for q in range(8):
-                first = 32 * (q // 4) + q % 4
+            nc.vector.memset(w_scales[s][:].bitcast(I32), 0)
+            for r in range(4):
                 nc.sync.dma_start(
-                    out=w_scales[first:P:64, :, s * STRIPE : (s + 1) * STRIPE].bitcast(I32),
-                    in_=scales_in[q:16:8, :, s * STRIPE // 4 : (s + 1) * STRIPE // 4],
+                    out=w_scales[s][r:P:32, :, :].bitcast(I32),
+                    in_=scales_in[r:16:4, :, s * STRIPE // 4 : (s + 1) * STRIPE // 4],
                 )
-            nc.sync.dma_start(
-                out=w_words[:, :, 2 * s * STRIPE : 2 * (s + 1) * STRIPE].bitcast(I32),
-                in_=words_in[:, :, s * STRIPE // 2 : (s + 1) * STRIPE // 2],
-            )
+            for c in range(s * STRIPE_BANKS, (s + 1) * STRIPE_BANKS):
+                nc.sync.dma_start(
+                    out=w_words[c][:].bitcast(I32),
+                    in_=words_in[:, :, c * BANK // 2 : (c + 1) * BANK // 2],
+                )
 
         def quantise_x(t):
             x_words = x_sb[t][:].bitcast(F32)
@@ -183,32 +196,29 @@ def tile_multiheadlatentattention_pb_kernel(tc, x, Wq_words, Wq_scales, out):
                     in_=flipped[:].rearrange("p (g u) m -> p g m u", u=2),
                 )
             nc.vector.quantize_mx(
-                out=x_codes[:, t, :].bitcast(FP8X4), scales=x_scales[:, t, :], in_=grouped[:]
+                out=x_codes[t][:].bitcast(FP8X4), scales=x_scales[t][:], in_=grouped[:]
             )
 
         def project(t, s):
             half = t % (SEQ // P)
             even_table = by_even[:, half, :, :].unsqueeze(1).to_broadcast([P, BANK_HEADS, PAIRS, 2])
             odd_table = by_odd[:, half, :, :].unsqueeze(1).to_broadcast([P, BANK_HEADS, PAIRS, 2])
-            result = results.tile([P, STRIPE], F32)
-            for b in range(STRIPE // BANK):
-                c = s * STRIPE + b * BANK
+            for b in range(STRIPE_BANKS):
+                c = s * STRIPE_BANKS + b
                 acc = psum_q.tile([P, BANK], F32)
                 for g in range(PASSES):
                     nc.tensor.matmul_mx(
                         out=acc[:],
-                        lhsT=x_codes[:, t, g * P : (g + 1) * P].bitcast(FP8X4),
-                        lhsT_scale=x_scales[:, t, g * P : (g + 1) * P],
-                        rhs=w_words[:, g, 2 * c : 2 * (c + BANK)].bitcast(FP4X4),
-                        rhs_scale=w_scales[:, g, c : c + BANK],
+                        lhsT=x_codes[t][:, g * P : (g + 1) * P].bitcast(FP8X4),
+                        lhsT_scale=x_scales[t][:, g * P : (g + 1) * P],
+                        rhs=w_words[c][:, g, :].bitcast(FP4X4),
+                        rhs_scale=w_scales[s][:, g, b * BANK : (b + 1) * BANK],
                         start=(g == 0),
                         stop=(g == PASSES - 1),
                     )
                 heads = acc[:].rearrange("p (h f i e) -> p h f i e", h=BANK_HEADS, f=2, e=2)
-                res = result[:, b * BANK : (b + 1) * BANK].rearrange(
-                    "p (h f i e) -> p h f i e", h=BANK_HEADS, f=2, e=2
-                )
-                nc.scalar.copy(out=res[:, :, 0, :, :], in_=heads[:, :, 0, :, :])
+                result = results.tile([P, BANK], F32)
+                res = result[:].rearrange("p (h f i e) -> p h f i e", h=BANK_HEADS, f=2, e=2)
                 from_odd = work.tile([P, BANK_HEADS, PAIRS, 2], F32)
                 nc.vector.tensor_tensor(
                     out=res[:, :, 1, :, :],
@@ -225,14 +235,16 @@ def tile_multiheadlatentattention_pb_kernel(tc, x, Wq_words, Wq_scales, out):
                 nc.gpsimd.tensor_tensor(
                     out=res[:, :, 1, :, :], in0=res[:, :, 1, :, :], in1=from_odd[:], op=ALU.add
                 )
-            nc.sync.dma_start(
-                out=out_rows[t * P : (t + 1) * P, s * STRIPE : (s + 1) * STRIPE], in_=result[:]
-            )
+                nc.scalar.copy(out=res[:, :, 0, :, :], in_=heads[:, :, 0, :, :])
+                nc.sync.dma_start(
+                    out=out_rows[t * P : (t + 1) * P, c * BANK : (c + 1) * BANK], in_=result[:]
+                )
 
         load_x(0)
+        load_x(1)
         load_weight_stripe(0)
-        for t in range(1, TOKEN_TILES):
-            load_x(t)
+        load_x(2)
+        load_x(3)
 
         identity = keep.tile([P, P], F32)
         make_identity(nc, identity[:])

@@ -199,11 +199,11 @@ def tile_multiheadlatentattention_pb_kernel(tc, x, Wq_words, Wq_scales, out):
                 out=x_codes[t][:].bitcast(FP8X4), scales=x_scales[t][:], in_=grouped[:]
             )
 
-        def project(t, s):
+        def project(t, s, banks=STRIPE_BANKS):
             half = t % (SEQ // P)
             even_table = by_even[:, half, :, :].unsqueeze(1).to_broadcast([P, BANK_HEADS, PAIRS, 2])
             odd_table = by_odd[:, half, :, :].unsqueeze(1).to_broadcast([P, BANK_HEADS, PAIRS, 2])
-            for b in range(STRIPE_BANKS):
+            for b in range(banks):
                 c = s * STRIPE_BANKS + b
                 acc = psum_q.tile([P, BANK], F32)
                 for g in range(PASSES):
@@ -240,6 +240,53 @@ def tile_multiheadlatentattention_pb_kernel(tc, x, Wq_words, Wq_scales, out):
                     out=out_rows[t * P : (t + 1) * P, c * BANK : (c + 1) * BANK], in_=result[:]
                 )
 
+        def project_last(t, s, b):
+            half = t % (SEQ // P)
+            c = s * STRIPE_BANKS + b
+            result = results.tile([P, BANK], F32)
+            res = result[:].rearrange("p (h f i e) -> p h f i e", h=BANK_HEADS, f=2, e=2)
+            out_heads = out_rows[t * P : (t + 1) * P, c * BANK : (c + 1) * BANK].rearrange(
+                "p (h f d) -> p h f d", h=BANK_HEADS, f=2
+            )
+            res_heads = result[:].rearrange("p (h f d) -> p h f d", h=BANK_HEADS, f=2)
+            for f in (1, 0):
+                acc = psum_q.tile([P, BANK_HEADS, PAIRS, 2], F32)
+                for h in range(BANK_HEADS):
+                    first = (2 * h + f) * 2 * PAIRS
+                    for g in range(PASSES):
+                        nc.tensor.matmul_mx(
+                            out=acc[:, h, :, :].rearrange("p i e -> p (i e)"),
+                            lhsT=x_codes[t][:, g * P : (g + 1) * P].bitcast(FP8X4),
+                            lhsT_scale=x_scales[t][:, g * P : (g + 1) * P],
+                            rhs=w_words[c][:, g, 2 * first : 2 * (first + 2 * PAIRS)].bitcast(FP4X4),
+                            rhs_scale=w_scales[s][
+                                :, g, b * BANK + first : b * BANK + first + 2 * PAIRS
+                            ],
+                            start=(g == 0),
+                            stop=(g == PASSES - 1),
+                        )
+                if f == 1:
+                    shape = [P, BANK_HEADS, PAIRS, 2]
+                    from_odd = work.tile(shape, F32)
+                    nc.vector.tensor_tensor(
+                        out=res[:, :, 1, :, :],
+                        in0=acc[:, :, :, 0:1].to_broadcast(shape),
+                        in1=by_even[:, half, :, :].unsqueeze(1).to_broadcast(shape),
+                        op=ALU.mult,
+                    )
+                    nc.vector.tensor_tensor(
+                        out=from_odd[:],
+                        in0=acc[:, :, :, 1:2].to_broadcast(shape),
+                        in1=by_odd[:, half, :, :].unsqueeze(1).to_broadcast(shape),
+                        op=ALU.mult,
+                    )
+                    nc.vector.tensor_tensor(
+                        out=res[:, :, 1, :, :], in0=res[:, :, 1, :, :], in1=from_odd[:], op=ALU.add
+                    )
+                else:
+                    nc.scalar.copy(out=res[:, :, 0, :, :], in_=acc[:])
+                nc.sync.dma_start(out=out_heads[:, :, f, :], in_=res_heads[:, :, f, :])
+
         load_x(0)
         load_x(1)
         load_weight_stripe(0)
@@ -260,4 +307,8 @@ def tile_multiheadlatentattention_pb_kernel(tc, x, Wq_words, Wq_scales, out):
             project(t, 0)
         for s in range(1, STRIPES):
             for t in range(TOKEN_TILES):
-                project(t, s)
+                if (s, t) == (STRIPES - 1, TOKEN_TILES - 1):
+                    project(t, s, STRIPE_BANKS - 1)
+                    project_last(t, s, STRIPE_BANKS - 1)
+                else:
+                    project(t, s)

@@ -136,11 +136,13 @@ def tile_multiheadlatentattention_pb_kernel(tc, x, Wq_words, Wq_scales, out):
 
     with ExitStack() as ctx:
         keep = ctx.enter_context(tc.tile_pool(name="keep", bufs=1))
-        stage = ctx.enter_context(tc.tile_pool(name="stage", bufs=2))
+        stage = ctx.enter_context(tc.tile_pool(name="stage", bufs=TOKEN_TILES))
         work = ctx.enter_context(tc.tile_pool(name="work", bufs=4))
         results = ctx.enter_context(tc.tile_pool(name="results", bufs=12))
-        psum_x = ctx.enter_context(tc.psum_pool(name="psum_x", bufs=2))
-        psum_q = ctx.enter_context(tc.psum_pool(name="psum_q", bufs=6))
+        psum = ctx.enter_context(tc.psum_pool(name="psum", bufs=8))
+        ctx.enter_context(
+            tc.manual_schedule(engines={mybir.EngineType.PE, mybir.EngineType.Pool})
+        )
 
         x_sb = [keep.tile([P, D_MODEL], BF16, name="x_sb%d" % t) for t in range(TOKEN_TILES)]
         x_codes = [
@@ -183,7 +185,7 @@ def tile_multiheadlatentattention_pb_kernel(tc, x, Wq_words, Wq_scales, out):
                 "p (g m u) -> p g m u", g=PASSES, u=2
             )
             for b in range(2):
-                flipped = psum_x.tile([P, 4, P], F32)
+                flipped = psum.tile([P, 4, P], F32, name="bank")
                 for j in range(4):
                     g, u = 2 * b + j // 2, j % 2
                     nc.tensor.transpose(
@@ -199,13 +201,13 @@ def tile_multiheadlatentattention_pb_kernel(tc, x, Wq_words, Wq_scales, out):
                 out=x_codes[t][:].bitcast(FP8X4), scales=x_scales[t][:], in_=grouped[:]
             )
 
-        def project(t, s, banks=STRIPE_BANKS):
+        def project(t, s, banks):
             half = t % (SEQ // P)
             even_table = by_even[:, half, :, :].unsqueeze(1).to_broadcast([P, BANK_HEADS, PAIRS, 2])
             odd_table = by_odd[:, half, :, :].unsqueeze(1).to_broadcast([P, BANK_HEADS, PAIRS, 2])
-            for b in range(banks):
+            for b in banks:
                 c = s * STRIPE_BANKS + b
-                acc = psum_q.tile([P, BANK], F32)
+                acc = psum.tile([P, BANK], F32, name="bank")
                 for g in range(PASSES):
                     nc.tensor.matmul_mx(
                         out=acc[:],
@@ -250,7 +252,7 @@ def tile_multiheadlatentattention_pb_kernel(tc, x, Wq_words, Wq_scales, out):
             )
             res_heads = result[:].rearrange("p (h f d) -> p h f d", h=BANK_HEADS, f=2)
             for f in (1, 0):
-                acc = psum_q.tile([P, BANK_HEADS, PAIRS, 2], F32)
+                acc = psum.tile([P, BANK_HEADS, PAIRS, 2], F32, name="bank")
                 for h in range(BANK_HEADS):
                     first = (2 * h + f) * 2 * PAIRS
                     for g in range(PASSES):
@@ -287,28 +289,37 @@ def tile_multiheadlatentattention_pb_kernel(tc, x, Wq_words, Wq_scales, out):
                     nc.scalar.copy(out=res[:, :, 0, :, :], in_=acc[:])
                 nc.sync.dma_start(out=out_heads[:, :, f, :], in_=res_heads[:, :, f, :])
 
-        load_x(0)
-        load_x(1)
-        load_weight_stripe(0)
-        load_x(2)
-        load_x(3)
+        zero_words = keep.tile([P, BANK // 2], F32)
+        nc.gpsimd.memset(zero_words[:], 0.0)
+        zeros = zero_words[:].bitcast(BF16)
+        idle_sums = psum.tile([P, BANK], F32, name="bank")
+
+        def keep_warm(count):
+            for i in range(count):
+                nc.tensor.matmul(idle_sums[:], lhsT=zeros[:, 0:P], rhs=zeros, start=True, stop=True)
+
+        keep_warm(4)
+
+        for t in range(TOKEN_TILES):
+            load_x(t)
+        for s in range(STRIPES):
+            load_weight_stripe(s)
 
         identity = keep.tile([P, P], F32)
         make_identity(nc, identity[:])
         by_even, by_odd = build_rope_tables(nc, keep)
 
-        quantise_x(0)
-        for s in range(1, STRIPES):
-            load_weight_stripe(s)
-
         for t in range(TOKEN_TILES):
-            if t + 1 < TOKEN_TILES:
-                quantise_x(t + 1)
-            project(t, 0)
+            quantise_x(t)
+            keep_warm(1 if t + 1 < TOKEN_TILES else 3)
+
+        for b in range(STRIPE_BANKS):
+            for t in range(TOKEN_TILES):
+                project(t, 0, [b])
         for s in range(1, STRIPES):
             for t in range(TOKEN_TILES):
                 if (s, t) == (STRIPES - 1, TOKEN_TILES - 1):
-                    project(t, s, STRIPE_BANKS - 1)
+                    project(t, s, [0])
                     project_last(t, s, STRIPE_BANKS - 1)
                 else:
-                    project(t, s)
+                    project(t, s, [0, 1])

@@ -144,21 +144,27 @@ def tile_multiheadlatentattention_pb_kernel(tc, x, Wq_words, Wq_scales, out):
             tc.manual_schedule(engines={mybir.EngineType.PE, mybir.EngineType.Pool})
         )
 
+        def starting_at(start, dtype, size, columns, name):
+            tile = keep.tile([P, columns + start // size], dtype, name=name, align_bytes=256)
+            return tile[:, start // size :]
+
         x_sb = [keep.tile([P, D_MODEL], BF16, name="x_sb%d" % t) for t in range(TOKEN_TILES)]
         x_codes = [
-            keep.tile([P, PASSES * P], U32, name="x_codes%d" % t, align_bytes=64)
-            for t in range(TOKEN_TILES)
+            starting_at(64, U32, 4, PASSES * P, "x_codes%d" % t) for t in range(TOKEN_TILES)
         ]
         x_scales = [
-            keep.tile([P, PASSES * P], U8, name="x_scales%d" % t, align_bytes=64)
-            for t in range(TOKEN_TILES)
+            starting_at(192, U8, 1, PASSES * P, "x_scales%d" % t) for t in range(TOKEN_TILES)
         ]
         w_words = [
-            keep.tile([P, PASSES, 2 * BANK], U8, name="w_words%d" % c, align_bytes=64)
+            starting_at(0, U8, 1, PASSES * 2 * BANK, "w_words%d" % c).rearrange(
+                "p (g n) -> p g n", g=PASSES
+            )
             for c in range(D_OUT // BANK)
         ]
         w_scales = [
-            keep.tile([P, PASSES, STRIPE], U8, name="w_scales%d" % s, align_bytes=64)
+            starting_at(128, U8, 1, PASSES * STRIPE, "w_scales%d" % s).rearrange(
+                "p (g n) -> p g n", g=PASSES
+            )
             for s in range(STRIPES)
         ]
 
@@ -166,7 +172,7 @@ def tile_multiheadlatentattention_pb_kernel(tc, x, Wq_words, Wq_scales, out):
             nc.sync.dma_start(out=x_sb[t][:], in_=x_rows[t * P : (t + 1) * P, :])
 
         def load_weight_stripe(s):
-            nc.vector.memset(w_scales[s][:].bitcast(I32), 0)
+            nc.vector.memset(w_scales[s].bitcast(I32), 0)
             for r in range(4):
                 nc.sync.dma_start(
                     out=w_scales[s][r:P:32, :, :].bitcast(I32),
@@ -174,7 +180,7 @@ def tile_multiheadlatentattention_pb_kernel(tc, x, Wq_words, Wq_scales, out):
                 )
             for c in range(s * STRIPE_BANKS, (s + 1) * STRIPE_BANKS):
                 nc.sync.dma_start(
-                    out=w_words[c][:].bitcast(I32),
+                    out=w_words[c].bitcast(I32),
                     in_=words_in[:, :, c * BANK // 2 : (c + 1) * BANK // 2],
                 )
 
@@ -198,7 +204,7 @@ def tile_multiheadlatentattention_pb_kernel(tc, x, Wq_words, Wq_scales, out):
                     in_=flipped[:].rearrange("p (g u) m -> p g m u", u=2),
                 )
             nc.vector.quantize_mx(
-                out=x_codes[t][:].bitcast(FP8X4), scales=x_scales[t][:], in_=grouped[:]
+                out=x_codes[t].bitcast(FP8X4), scales=x_scales[t], in_=grouped[:]
             )
 
         def project(t, s, banks):

@@ -28,9 +28,8 @@ PASSES = D_MODEL // K_PASS
 TOKEN_TILES = TOKENS // P
 BANK = 512
 BANK_HEADS = BANK // HEAD
-STRIPE_BANKS = 2
-STRIPE = STRIPE_BANKS * BANK
-STRIPES = D_OUT // STRIPE
+STRIPE_BANKS = (1, 1, 2, 4)
+STRIPES = len(STRIPE_BANKS)
 
 FLOPS = 2 * TOKENS * D_MODEL * D_OUT
 
@@ -156,13 +155,13 @@ def tile_multiheadlatentattention_pb_kernel(tc, x, Wq_words, Wq_scales, out):
             starting_at(192, U8, 1, PASSES * P, "x_scales%d" % t) for t in range(TOKEN_TILES)
         ]
         w_words = [
-            starting_at(0, U8, 1, PASSES * 2 * BANK, "w_words%d" % c).rearrange(
+            starting_at(0, U8, 1, PASSES * 2 * BANK * STRIPE_BANKS[s], "w_words%d" % s).rearrange(
                 "p (g n) -> p g n", g=PASSES
             )
-            for c in range(D_OUT // BANK)
+            for s in range(STRIPES)
         ]
         w_scales = [
-            starting_at(128, U8, 1, PASSES * STRIPE, "w_scales%d" % s).rearrange(
+            starting_at(128, U8, 1, PASSES * BANK * STRIPE_BANKS[s], "w_scales%d" % s).rearrange(
                 "p (g n) -> p g n", g=PASSES
             )
             for s in range(STRIPES)
@@ -172,17 +171,17 @@ def tile_multiheadlatentattention_pb_kernel(tc, x, Wq_words, Wq_scales, out):
             nc.sync.dma_start(out=x_sb[t][:], in_=x_rows[t * P : (t + 1) * P, :])
 
         def load_weight_stripe(s):
+            first = sum(STRIPE_BANKS[:s]) * BANK
+            width = STRIPE_BANKS[s] * BANK
             nc.vector.memset(w_scales[s].bitcast(I32), 0)
             for r in range(4):
                 nc.sync.dma_start(
                     out=w_scales[s][r:P:32, :, :].bitcast(I32),
-                    in_=scales_in[r:16:4, :, s * STRIPE // 4 : (s + 1) * STRIPE // 4],
+                    in_=scales_in[r:16:4, :, first // 4 : (first + width) // 4],
                 )
-            for c in range(s * STRIPE_BANKS, (s + 1) * STRIPE_BANKS):
-                nc.sync.dma_start(
-                    out=w_words[c].bitcast(I32),
-                    in_=words_in[:, :, c * BANK // 2 : (c + 1) * BANK // 2],
-                )
+            nc.sync.dma_start(
+                out=w_words[s].bitcast(I32), in_=words_in[:, :, first // 2 : (first + width) // 2]
+            )
 
         def quantise_x(t):
             x_words = x_sb[t][:].bitcast(F32)
@@ -212,14 +211,14 @@ def tile_multiheadlatentattention_pb_kernel(tc, x, Wq_words, Wq_scales, out):
             even_table = by_even[:, half, :, :].unsqueeze(1).to_broadcast([P, BANK_HEADS, PAIRS, 2])
             odd_table = by_odd[:, half, :, :].unsqueeze(1).to_broadcast([P, BANK_HEADS, PAIRS, 2])
             for b in banks:
-                c = s * STRIPE_BANKS + b
+                c = sum(STRIPE_BANKS[:s]) + b
                 acc = psum.tile([P, BANK], F32, name="bank")
                 for g in range(PASSES):
                     nc.tensor.matmul_mx(
                         out=acc[:],
                         lhsT=x_codes[t][:, g * P : (g + 1) * P].bitcast(FP8X4),
                         lhsT_scale=x_scales[t][:, g * P : (g + 1) * P],
-                        rhs=w_words[c][:, g, :].bitcast(FP4X4),
+                        rhs=w_words[s][:, g, 2 * b * BANK : 2 * (b + 1) * BANK].bitcast(FP4X4),
                         rhs_scale=w_scales[s][:, g, b * BANK : (b + 1) * BANK],
                         start=(g == 0),
                         stop=(g == PASSES - 1),
@@ -250,7 +249,7 @@ def tile_multiheadlatentattention_pb_kernel(tc, x, Wq_words, Wq_scales, out):
 
         def project_last(t, s, b):
             half = t % (SEQ // P)
-            c = s * STRIPE_BANKS + b
+            c = sum(STRIPE_BANKS[:s]) + b
             result = results.tile([P, BANK], F32)
             res = result[:].rearrange("p (h f i e) -> p h f i e", h=BANK_HEADS, f=2, e=2)
             out_heads = out_rows[t * P : (t + 1) * P, c * BANK : (c + 1) * BANK].rearrange(
@@ -260,16 +259,14 @@ def tile_multiheadlatentattention_pb_kernel(tc, x, Wq_words, Wq_scales, out):
             for f in (1, 0):
                 acc = psum.tile([P, BANK_HEADS, PAIRS, 2], F32, name="bank")
                 for h in range(BANK_HEADS):
-                    first = (2 * h + f) * 2 * PAIRS
+                    first = b * BANK + (2 * h + f) * 2 * PAIRS
                     for g in range(PASSES):
                         nc.tensor.matmul_mx(
                             out=acc[:, h, :, :].rearrange("p i e -> p (i e)"),
                             lhsT=x_codes[t][:, g * P : (g + 1) * P].bitcast(FP8X4),
                             lhsT_scale=x_scales[t][:, g * P : (g + 1) * P],
-                            rhs=w_words[c][:, g, 2 * first : 2 * (first + 2 * PAIRS)].bitcast(FP4X4),
-                            rhs_scale=w_scales[s][
-                                :, g, b * BANK + first : b * BANK + first + 2 * PAIRS
-                            ],
+                            rhs=w_words[s][:, g, 2 * first : 2 * (first + 2 * PAIRS)].bitcast(FP4X4),
+                            rhs_scale=w_scales[s][:, g, first : first + 2 * PAIRS],
                             start=(g == 0),
                             stop=(g == PASSES - 1),
                         )
@@ -319,13 +316,10 @@ def tile_multiheadlatentattention_pb_kernel(tc, x, Wq_words, Wq_scales, out):
             quantise_x(t)
             keep_warm(1 if t + 1 < TOKEN_TILES else 3)
 
-        for b in range(STRIPE_BANKS):
-            for t in range(TOKEN_TILES):
-                project(t, 0, [b])
-        for s in range(1, STRIPES):
+        for s in range(STRIPES):
             for t in range(TOKEN_TILES):
                 if (s, t) == (STRIPES - 1, TOKEN_TILES - 1):
-                    project(t, s, [0])
-                    project_last(t, s, STRIPE_BANKS - 1)
+                    project(t, s, range(STRIPE_BANKS[s] - 1))
+                    project_last(t, s, STRIPE_BANKS[s] - 1)
                 else:
-                    project(t, s, [0, 1])
+                    project(t, s, range(STRIPE_BANKS[s]))

@@ -147,7 +147,13 @@ def tile_multiheadlatentattention_pb_kernel(tc, x, Wq_words, Wq_scales, out):
             tile = keep.tile([P, columns + start // size], dtype, name=name, align_bytes=256)
             return tile[:, start // size :]
 
-        x_sb = [keep.tile([P, D_MODEL], BF16, name="x_sb%d" % t) for t in range(TOKEN_TILES)]
+        x_sb = [
+            [
+                keep.tile([P, D_MODEL // loads], BF16, name="x_sb%d_%d" % (t, i))
+                for i in range(loads)
+            ]
+            for t, loads in enumerate([2] + (TOKEN_TILES - 1) * [1])
+        ]
         x_codes = [
             starting_at(64, U32, 4, PASSES * P, "x_codes%d" % t) for t in range(TOKEN_TILES)
         ]
@@ -168,7 +174,11 @@ def tile_multiheadlatentattention_pb_kernel(tc, x, Wq_words, Wq_scales, out):
         ]
 
         def load_x(t):
-            nc.sync.dma_start(out=x_sb[t][:], in_=x_rows[t * P : (t + 1) * P, :])
+            width = D_MODEL // len(x_sb[t])
+            for i, part in enumerate(x_sb[t]):
+                nc.sync.dma_start(
+                    out=part[:], in_=x_rows[t * P : (t + 1) * P, i * width : (i + 1) * width]
+                )
 
         def load_weight_stripe(s):
             first = sum(STRIPE_BANKS[:s]) * BANK
@@ -184,18 +194,20 @@ def tile_multiheadlatentattention_pb_kernel(tc, x, Wq_words, Wq_scales, out):
             )
 
         def quantise_x(t):
-            x_words = x_sb[t][:].bitcast(F32)
             grouped = stage.tile([P, D_MODEL], BF16, align_bytes=64)
             grouped_words = grouped[:].bitcast(F32).rearrange(
                 "p (g m u) -> p g m u", g=PASSES, u=2
             )
             for b in range(2):
                 flipped = psum.tile([P, 4, P], F32, name="bank")
+                i = b * len(x_sb[t]) // 2
+                x_words = x_sb[t][i][:].bitcast(F32)
                 for j in range(4):
                     g, u = 2 * b + j // 2, j % 2
+                    first = 256 * g - i * (D_MODEL // 2 // len(x_sb[t]))
                     nc.tensor.transpose(
                         flipped[:, j, :],
-                        x_words[:, 256 * g + u : 256 * (g + 1) : 2],
+                        x_words[:, first + u : first + 256 : 2],
                         identity[:],
                     )
                 nc.scalar.copy(
@@ -205,6 +217,9 @@ def tile_multiheadlatentattention_pb_kernel(tc, x, Wq_words, Wq_scales, out):
             nc.vector.quantize_mx(
                 out=x_codes[t].bitcast(FP8X4), scales=x_scales[t], in_=grouped[:]
             )
+
+        def words_of(s, g):
+            return w_words[s][:, g, :]
 
         def project(t, s, banks):
             half = t % (SEQ // P)
@@ -218,7 +233,7 @@ def tile_multiheadlatentattention_pb_kernel(tc, x, Wq_words, Wq_scales, out):
                         out=acc[:],
                         lhsT=x_codes[t][:, g * P : (g + 1) * P].bitcast(FP8X4),
                         lhsT_scale=x_scales[t][:, g * P : (g + 1) * P],
-                        rhs=w_words[s][:, g, 2 * b * BANK : 2 * (b + 1) * BANK].bitcast(FP4X4),
+                        rhs=words_of(s, g)[:, 2 * b * BANK : 2 * (b + 1) * BANK].bitcast(FP4X4),
                         rhs_scale=w_scales[s][:, g, b * BANK : (b + 1) * BANK],
                         start=(g == 0),
                         stop=(g == PASSES - 1),
@@ -247,50 +262,69 @@ def tile_multiheadlatentattention_pb_kernel(tc, x, Wq_words, Wq_scales, out):
                     out=out_rows[t * P : (t + 1) * P, c * BANK : (c + 1) * BANK], in_=result[:]
                 )
 
-        def project_last(t, s, b):
+        def project_last(t, s):
             half = t % (SEQ // P)
-            c = sum(STRIPE_BANKS[:s]) + b
-            result = results.tile([P, BANK], F32)
-            res = result[:].rearrange("p (h f i e) -> p h f i e", h=BANK_HEADS, f=2, e=2)
-            out_heads = out_rows[t * P : (t + 1) * P, c * BANK : (c + 1) * BANK].rearrange(
-                "p (h f d) -> p h f d", h=BANK_HEADS, f=2
-            )
-            res_heads = result[:].rearrange("p (h f d) -> p h f d", h=BANK_HEADS, f=2)
-            for f in (1, 0):
-                acc = psum.tile([P, BANK_HEADS, PAIRS, 2], F32, name="bank")
+            shape = [P, BANK_HEADS, PAIRS, 2]
+            even_table = by_even[:, half, :, :].unsqueeze(1).to_broadcast(shape)
+            odd_table = by_odd[:, half, :, :].unsqueeze(1).to_broadcast(shape)
+            banks = range(STRIPE_BANKS[s] - 2, STRIPE_BANKS[s])
+            res = {b: results.tile([P, BANK_HEADS, 2, PAIRS, 2], F32, name="result") for b in banks}
+
+            def half_head(acc, b, h, f):
+                first = b * BANK + (2 * h + f) * 2 * PAIRS
+                for g in range(PASSES):
+                    nc.tensor.matmul_mx(
+                        out=acc.rearrange("p i e -> p (i e)"),
+                        lhsT=x_codes[t][:, g * P : (g + 1) * P].bitcast(FP8X4),
+                        lhsT_scale=x_scales[t][:, g * P : (g + 1) * P],
+                        rhs=words_of(s, g)[:, 2 * first : 2 * (first + 2 * PAIRS)].bitcast(FP4X4),
+                        rhs_scale=w_scales[s][:, g, first : first + 2 * PAIRS],
+                        start=(g == 0),
+                        stop=(g == PASSES - 1),
+                    )
+
+            def store(b, heads, f):
+                c = sum(STRIPE_BANKS[:s]) + b
+                out_heads = out_rows[t * P : (t + 1) * P, c * BANK : (c + 1) * BANK].rearrange(
+                    "p (h f i e) -> p h f i e", h=BANK_HEADS, f=2, e=2
+                )
+                nc.sync.dma_start(out=out_heads[:, heads, f, :, :], in_=res[b][:, heads, f, :, :])
+
+            for b in banks:
+                acc = psum.tile(shape, F32, name="bank")
                 for h in range(BANK_HEADS):
-                    first = b * BANK + (2 * h + f) * 2 * PAIRS
-                    for g in range(PASSES):
-                        nc.tensor.matmul_mx(
-                            out=acc[:, h, :, :].rearrange("p i e -> p (i e)"),
-                            lhsT=x_codes[t][:, g * P : (g + 1) * P].bitcast(FP8X4),
-                            lhsT_scale=x_scales[t][:, g * P : (g + 1) * P],
-                            rhs=w_words[s][:, g, 2 * first : 2 * (first + 2 * PAIRS)].bitcast(FP4X4),
-                            rhs_scale=w_scales[s][:, g, first : first + 2 * PAIRS],
-                            start=(g == 0),
-                            stop=(g == PASSES - 1),
-                        )
-                if f == 1:
-                    shape = [P, BANK_HEADS, PAIRS, 2]
-                    from_odd = work.tile(shape, F32)
-                    nc.vector.tensor_tensor(
-                        out=res[:, :, 1, :, :],
-                        in0=acc[:, :, :, 0:1].to_broadcast(shape),
-                        in1=by_even[:, half, :, :].unsqueeze(1).to_broadcast(shape),
-                        op=ALU.mult,
-                    )
-                    nc.vector.tensor_tensor(
-                        out=from_odd[:],
-                        in0=acc[:, :, :, 1:2].to_broadcast(shape),
-                        in1=by_odd[:, half, :, :].unsqueeze(1).to_broadcast(shape),
-                        op=ALU.mult,
-                    )
-                    nc.vector.tensor_tensor(
-                        out=res[:, :, 1, :, :], in0=res[:, :, 1, :, :], in1=from_odd[:], op=ALU.add
-                    )
-                else:
-                    nc.scalar.copy(out=res[:, :, 0, :, :], in_=acc[:])
-                nc.sync.dma_start(out=out_heads[:, :, f, :], in_=res_heads[:, :, f, :])
+                    half_head(acc[:, h, :, :], b, h, 1)
+                rotated = res[b][:, :, 1, :, :]
+                from_odd = work.tile(shape, F32)
+                nc.vector.tensor_tensor(
+                    out=rotated,
+                    in0=acc[:, :, :, 0:1].to_broadcast(shape),
+                    in1=even_table,
+                    op=ALU.mult,
+                )
+                nc.vector.tensor_tensor(
+                    out=from_odd[:],
+                    in0=acc[:, :, :, 1:2].to_broadcast(shape),
+                    in1=odd_table,
+                    op=ALU.mult,
+                )
+                adder = nc.gpsimd if b == banks[0] else nc.vector
+                adder.tensor_tensor(out=rotated, in0=rotated, in1=from_odd[:], op=ALU.add)
+                store(b, slice(0, BANK_HEADS), 1)
+
+            b = banks[0]
+            acc = psum.tile(shape, F32, name="bank")
+            for h in range(BANK_HEADS):
+                half_head(acc[:, h, :, :], b, h, 0)
+            nc.scalar.copy(out=res[b][:, :, 0, :, :], in_=acc[:])
+            store(b, slice(0, BANK_HEADS), 0)
+
+            b = banks[1]
+            for h, copy in enumerate((nc.scalar.copy, nc.vector.tensor_copy)):
+                acc = psum.tile([P, PAIRS, 2], F32, name="bank")
+                half_head(acc[:], b, h, 0)
+                copy(out=res[b][:, h, 0, :, :], in_=acc[:])
+                store(b, slice(h, h + 1), 0)
 
         zero_words = keep.tile([P, BANK // 2], F32)
         nc.gpsimd.memset(zero_words[:], 0.0)
@@ -319,7 +353,7 @@ def tile_multiheadlatentattention_pb_kernel(tc, x, Wq_words, Wq_scales, out):
         for s in range(STRIPES):
             for t in range(TOKEN_TILES):
                 if (s, t) == (STRIPES - 1, TOKEN_TILES - 1):
-                    project(t, s, range(STRIPE_BANKS[s] - 1))
-                    project_last(t, s, STRIPE_BANKS[s] - 1)
+                    project(t, s, range(STRIPE_BANKS[s] - 2))
+                    project_last(t, s)
                 else:
                     project(t, s, range(STRIPE_BANKS[s]))

@@ -35,25 +35,22 @@ FLOPS = 2 * TOKENS * D_MODEL * D_OUT
 
 ROUND_MAGIC = 1.5 * 2.0**23
 PI_HI = 3.140625
-PI_MID = round((math.pi - PI_HI) * 2.0**22) / 2.0**22
-PI_LO = math.pi - PI_HI - PI_MID
+PI_LO = math.pi - PI_HI
 
 
-def build_rope_tables(nc, pool):
-    warm = pool.tile([P, 1], F32)
-    nc.vector.memset(warm[:], 0.0)
-    nc.scalar.activation(out=warm[:], in_=warm[:], func=ACT.Sin)
-
+def reduce_angles(nc, pool, fill):
     freq = pool.tile([P, PAIRS], F32)
     nc.vector.memset(freq[:, 0:1], 1.0)
-    for done in (1, 2, 4, 8, 16, 32):
-        nc.vector.tensor_scalar(
-            out=freq[:, done : 2 * done],
-            in0=freq[:, 0:done],
-            scalar1=ROPE_BASE ** (-2.0 * done / (2 * PAIRS)),
-            scalar2=None,
-            op0=ALU.mult,
-        )
+    for done, other_work in zip((1, 4, 16), fill):
+        for k in (1, 2, 3):
+            nc.vector.tensor_scalar(
+                out=freq[:, k * done : (k + 1) * done],
+                in0=freq[:, 0:done],
+                scalar1=ROPE_BASE ** (-2.0 * k * done / (2 * PAIRS)),
+                scalar2=None,
+                op0=ALU.mult,
+            )
+        other_work()
 
     position_int = pool.tile([P, 2], I32)
     nc.gpsimd.iota(position_int[:], pattern=[[P, 2]], base=0, channel_multiplier=1)
@@ -83,33 +80,35 @@ def build_rope_tables(nc, pool):
     nc.vector.tensor_scalar(
         out=odd_n[:], in0=shifted[:].bitcast(I32), scalar1=1, scalar2=None, op0=ALU.bitwise_and
     )
-    sign = pool.tile([P, 2, PAIRS], F32)
-    nc.vector.tensor_scalar(
-        out=sign[:], in0=odd_n[:], scalar1=-2.0, scalar2=1.0, op0=ALU.mult, op1=ALU.add
-    )
     n = pool.tile([P, 2, PAIRS], F32)
     nc.vector.tensor_scalar(
         out=n[:], in0=shifted[:], scalar1=ROUND_MAGIC, scalar2=None, op0=ALU.subtract
+    )
+    sign = pool.tile([P, 2, PAIRS], F32)
+    nc.vector.tensor_scalar(
+        out=sign[:], in0=odd_n[:], scalar1=-2.0, scalar2=1.0, op0=ALU.mult, op1=ALU.add
     )
     rest = pool.tile([P, 2, PAIRS], F32)
     nc.vector.scalar_tensor_tensor(
         out=rest[:], in0=n[:], scalar=-PI_HI, in1=angle[:], op0=ALU.mult, op1=ALU.add
     )
-    for piece in (PI_MID, PI_LO):
-        nc.vector.scalar_tensor_tensor(
-            out=rest[:], in0=n[:], scalar=-piece, in1=rest[:], op0=ALU.mult, op1=ALU.add
-        )
+    nc.vector.scalar_tensor_tensor(
+        out=rest[:], in0=n[:], scalar=-PI_LO, in1=rest[:], op0=ALU.mult, op1=ALU.add
+    )
     rest_abs = pool.tile([P, 2, PAIRS], F32)
     nc.vector.scalar_tensor_tensor(
         out=rest_abs[:], in0=rest[:], scalar=-1.0, in1=rest[:], op0=ALU.mult, op1=ALU.max
     )
+    return rest, rest_abs, sign
+
+
+def build_rope_tables(nc, pool, rest, rest_abs, sign):
     sin_rest = pool.tile([P, 2, PAIRS], F32)
     nc.scalar.activation(out=sin_rest[:], in_=rest[:], func=ACT.Sin)
     cos_rest = pool.tile([P, 2, PAIRS], F32)
     nc.scalar.activation(
         out=cos_rest[:], in_=rest_abs[:], func=ACT.Sin, scale=-1.0, bias=math.pi / 2.0
     )
-
     by_even = pool.tile([P, 2, PAIRS, 2], F32)
     by_odd = pool.tile([P, 2, PAIRS, 2], F32)
     nc.vector.tensor_tensor(out=by_even[:, :, :, 0], in0=cos_rest[:], in1=sign[:], op=ALU.mult)
@@ -140,7 +139,9 @@ def tile_multiheadlatentattention_pb_kernel(tc, x, Wq_words, Wq_scales, out):
         results = ctx.enter_context(tc.tile_pool(name="results", bufs=12))
         psum = ctx.enter_context(tc.psum_pool(name="psum", bufs=8))
         ctx.enter_context(
-            tc.manual_schedule(engines={mybir.EngineType.PE, mybir.EngineType.Pool})
+            tc.manual_schedule(
+                engines={mybir.EngineType.PE, mybir.EngineType.Pool, mybir.EngineType.DVE}
+            )
         )
 
         def starting_at(start, dtype, size, columns, name):
@@ -180,10 +181,12 @@ def tile_multiheadlatentattention_pb_kernel(tc, x, Wq_words, Wq_scales, out):
                     out=part[:], in_=x_rows[t * P : (t + 1) * P, i * width : (i + 1) * width]
                 )
 
+        def zero_scales(s):
+            nc.vector.memset(w_scales[s].bitcast(I32), 0)
+
         def load_weight_stripe(s):
             first = sum(STRIPE_BANKS[:s]) * BANK
             width = STRIPE_BANKS[s] * BANK
-            nc.vector.memset(w_scales[s].bitcast(I32), 0)
             for r in range(4):
                 nc.sync.dma_start(
                     out=w_scales[s][r:P:32, :, :].bitcast(I32),
@@ -339,16 +342,28 @@ def tile_multiheadlatentattention_pb_kernel(tc, x, Wq_words, Wq_scales, out):
 
         for t in range(TOKEN_TILES):
             load_x(t)
-        for s in range(STRIPES):
-            load_weight_stripe(s)
-
         identity = keep.tile([P, P], F32)
         make_identity(nc, identity[:])
-        by_even, by_odd = build_rope_tables(nc, keep)
+
+        warm = keep.tile([P, 1], F32)
+        nc.vector.memset(warm[:], 0.0)
+        nc.scalar.activation(out=warm[:], in_=warm[:], func=ACT.Sin)
+
+        zero_scales(0)
+        load_weight_stripe(0)
+        reduced = reduce_angles(
+            nc, keep, [lambda: zero_scales(1), lambda: zero_scales(2), lambda: None]
+        )
+        load_weight_stripe(1)
+        load_weight_stripe(2)
 
         for t in range(TOKEN_TILES):
             quantise_x(t)
+            if t == 1:
+                zero_scales(3)
+                load_weight_stripe(3)
             keep_warm(1 if t + 1 < TOKEN_TILES else 3)
+        by_even, by_odd = build_rope_tables(nc, keep, *reduced)
 
         for s in range(STRIPES):
             for t in range(TOKEN_TILES):

import math
from contextlib import ExitStack

import concourse.mybir as mybir
from concourse.masks import make_identity

F32 = mybir.dt.float32
BF16 = mybir.dt.bfloat16
I32 = mybir.dt.int32
U32 = mybir.dt.uint32
U8 = mybir.dt.uint8
FP8X4 = mybir.dt.float8_e4m3fn_x4
FP4X4 = mybir.dt.float4_e2m1fn_x4
ALU = mybir.AluOpType
ACT = mybir.ActivationFunctionType

P = 128
TOKENS = 512
SEQ = 256
D_MODEL = 2048
D_OUT = 4096
HEAD = 256
PAIRS = 64
ROPE_BASE = 10000.0

K_PASS = 4 * P
PASSES = D_MODEL // K_PASS
TOKEN_TILES = TOKENS // P
BANK = 512
BANK_HEADS = BANK // HEAD
STRIPE_BANKS = (1, 1, 2, 4)
STRIPES = len(STRIPE_BANKS)

FLOPS = 2 * TOKENS * D_MODEL * D_OUT

ROUND_MAGIC = 1.5 * 2.0**23
PI_HI = 3.140625
PI_LO = math.pi - PI_HI


def reduce_angles(nc, pool, fill):
    freq = pool.tile([P, PAIRS], F32)
    nc.vector.memset(freq[:, 0:1], 1.0)
    for done, other_work in zip((1, 4, 16), fill):
        for k in (1, 2, 3):
            nc.vector.tensor_scalar(
                out=freq[:, k * done : (k + 1) * done],
                in0=freq[:, 0:done],
                scalar1=ROPE_BASE ** (-2.0 * k * done / (2 * PAIRS)),
                scalar2=None,
                op0=ALU.mult,
            )
        other_work()

    position_int = pool.tile([P, 2], I32)
    nc.gpsimd.iota(position_int[:], pattern=[[P, 2]], base=0, channel_multiplier=1)
    position = pool.tile([P, 2], F32)
    nc.vector.tensor_copy(out=position[:], in_=position_int[:])

    angle = pool.tile([P, 2, PAIRS], F32)
    for half in range(2):
        nc.vector.tensor_scalar(
            out=angle[:, half, :],
            in0=freq[:],
            scalar1=position[:, half : half + 1],
            scalar2=None,
            op0=ALU.mult,
        )

    shifted = pool.tile([P, 2, PAIRS], F32)
    nc.vector.tensor_scalar(
        out=shifted[:],
        in0=angle[:],
        scalar1=1.0 / math.pi,
        scalar2=ROUND_MAGIC,
        op0=ALU.mult,
        op1=ALU.add,
    )
    odd_n = pool.tile([P, 2, PAIRS], I32)
    nc.vector.tensor_scalar(
        out=odd_n[:], in0=shifted[:].bitcast(I32), scalar1=1, scalar2=None, op0=ALU.bitwise_and
    )
    n = pool.tile([P, 2, PAIRS], F32)
    nc.vector.tensor_scalar(
        out=n[:], in0=shifted[:], scalar1=ROUND_MAGIC, scalar2=None, op0=ALU.subtract
    )
    sign = pool.tile([P, 2, PAIRS], F32)
    nc.vector.tensor_scalar(
        out=sign[:], in0=odd_n[:], scalar1=-2.0, scalar2=1.0, op0=ALU.mult, op1=ALU.add
    )
    rest = pool.tile([P, 2, PAIRS], F32)
    nc.vector.scalar_tensor_tensor(
        out=rest[:], in0=n[:], scalar=-PI_HI, in1=angle[:], op0=ALU.mult, op1=ALU.add
    )
    nc.vector.scalar_tensor_tensor(
        out=rest[:], in0=n[:], scalar=-PI_LO, in1=rest[:], op0=ALU.mult, op1=ALU.add
    )
    rest_abs = pool.tile([P, 2, PAIRS], F32)
    nc.vector.scalar_tensor_tensor(
        out=rest_abs[:], in0=rest[:], scalar=-1.0, in1=rest[:], op0=ALU.mult, op1=ALU.max
    )
    return rest, rest_abs, sign


def build_rope_tables(nc, pool, rest, rest_abs, sign):
    sin_rest = pool.tile([P, 2, PAIRS], F32)
    nc.scalar.activation(out=sin_rest[:], in_=rest[:], func=ACT.Sin)
    cos_rest = pool.tile([P, 2, PAIRS], F32)
    nc.scalar.activation(
        out=cos_rest[:], in_=rest_abs[:], func=ACT.Sin, scale=-1.0, bias=math.pi / 2.0
    )
    by_even = pool.tile([P, 2, PAIRS, 2], F32)
    by_odd = pool.tile([P, 2, PAIRS, 2], F32)
    nc.vector.tensor_tensor(out=by_even[:, :, :, 0], in0=cos_rest[:], in1=sign[:], op=ALU.mult)
    nc.vector.tensor_tensor(out=by_even[:, :, :, 1], in0=sin_rest[:], in1=sign[:], op=ALU.mult)
    nc.vector.scalar_tensor_tensor(
        out=by_odd[:, :, :, 0],
        in0=sin_rest[:],
        scalar=-1.0,
        in1=sign[:],
        op0=ALU.mult,
        op1=ALU.mult,
    )
    nc.vector.tensor_tensor(out=by_odd[:, :, :, 1], in0=cos_rest[:], in1=sign[:], op=ALU.mult)
    return by_even, by_odd


def tile_multiheadlatentattention_pb_kernel(tc, x, Wq_words, Wq_scales, out):
    nc = tc.nc
    x_rows = x.flatten_outer_dims()
    out_rows = out.rearrange("b s h d -> (b s) (h d)")
    words_in = Wq_words.bitcast(I32).rearrange("g p n -> p g n")
    scales_in = Wq_scales.bitcast(I32).rearrange("g q n -> q g n")

    with ExitStack() as ctx:
        keep = ctx.enter_context(tc.tile_pool(name="keep", bufs=1))
        stage = ctx.enter_context(tc.tile_pool(name="stage", bufs=TOKEN_TILES))
        work = ctx.enter_context(tc.tile_pool(name="work", bufs=4))
        results = ctx.enter_context(tc.tile_pool(name="results", bufs=12))
        psum = ctx.enter_context(tc.psum_pool(name="psum", bufs=8))
        ctx.enter_context(
            tc.manual_schedule(
                engines={mybir.EngineType.PE, mybir.EngineType.Pool, mybir.EngineType.DVE}
            )
        )

        def starting_at(start, dtype, size, columns, name):
            tile = keep.tile([P, columns + start // size], dtype, name=name, align_bytes=256)
            return tile[:, start // size :]

        x_sb = [
            [
                keep.tile([P, D_MODEL // loads], BF16, name="x_sb%d_%d" % (t, i))
                for i in range(loads)
            ]
            for t, loads in enumerate([2] + (TOKEN_TILES - 1) * [1])
        ]
        x_codes = [
            starting_at(64, U32, 4, PASSES * P, "x_codes%d" % t) for t in range(TOKEN_TILES)
        ]
        x_scales = [
            starting_at(192, U8, 1, PASSES * P, "x_scales%d" % t) for t in range(TOKEN_TILES)
        ]
        w_words = [
            starting_at(0, U8, 1, PASSES * 2 * BANK * STRIPE_BANKS[s], "w_words%d" % s).rearrange(
                "p (g n) -> p g n", g=PASSES
            )
            for s in range(STRIPES)
        ]
        w_scales = [
            starting_at(128, U8, 1, PASSES * BANK * STRIPE_BANKS[s], "w_scales%d" % s).rearrange(
                "p (g n) -> p g n", g=PASSES
            )
            for s in range(STRIPES)
        ]

        def load_x(t):
            width = D_MODEL // len(x_sb[t])
            for i, part in enumerate(x_sb[t]):
                nc.sync.dma_start(
                    out=part[:], in_=x_rows[t * P : (t + 1) * P, i * width : (i + 1) * width]
                )

        def zero_scales(s):
            nc.vector.memset(w_scales[s].bitcast(I32), 0)

        def load_weight_stripe(s):
            first = sum(STRIPE_BANKS[:s]) * BANK
            width = STRIPE_BANKS[s] * BANK
            for r in range(4):
                nc.sync.dma_start(
                    out=w_scales[s][r:P:32, :, :].bitcast(I32),
                    in_=scales_in[r:16:4, :, first // 4 : (first + width) // 4],
                )
            nc.sync.dma_start(
                out=w_words[s].bitcast(I32), in_=words_in[:, :, first // 2 : (first + width) // 2]
            )

        def quantise_x(t):
            grouped = stage.tile([P, D_MODEL], BF16, align_bytes=64)
            grouped_words = grouped[:].bitcast(F32).rearrange(
                "p (g m u) -> p g m u", g=PASSES, u=2
            )
            for b in range(2):
                flipped = psum.tile([P, 4, P], F32, name="bank")
                i = b * len(x_sb[t]) // 2
                x_words = x_sb[t][i][:].bitcast(F32)
                for j in range(4):
                    g, u = 2 * b + j // 2, j % 2
                    first = 256 * g - i * (D_MODEL // 2 // len(x_sb[t]))
                    nc.tensor.transpose(
                        flipped[:, j, :],
                        x_words[:, first + u : first + 256 : 2],
                        identity[:],
                    )
                nc.scalar.copy(
                    out=grouped_words[:, 2 * b : 2 * b + 2, :, :],
                    in_=flipped[:].rearrange("p (g u) m -> p g m u", u=2),
                )
            nc.vector.quantize_mx(
                out=x_codes[t].bitcast(FP8X4), scales=x_scales[t], in_=grouped[:]
            )

        def words_of(s, g):
            return w_words[s][:, g, :]

        def project(t, s, banks):
            half = t % (SEQ // P)
            even_table = by_even[:, half, :, :].unsqueeze(1).to_broadcast([P, BANK_HEADS, PAIRS, 2])
            odd_table = by_odd[:, half, :, :].unsqueeze(1).to_broadcast([P, BANK_HEADS, PAIRS, 2])
            for b in banks:
                c = sum(STRIPE_BANKS[:s]) + b
                acc = psum.tile([P, BANK], F32, name="bank")
                for g in range(PASSES):
                    nc.tensor.matmul_mx(
                        out=acc[:],
                        lhsT=x_codes[t][:, g * P : (g + 1) * P].bitcast(FP8X4),
                        lhsT_scale=x_scales[t][:, g * P : (g + 1) * P],
                        rhs=words_of(s, g)[:, 2 * b * BANK : 2 * (b + 1) * BANK].bitcast(FP4X4),
                        rhs_scale=w_scales[s][:, g, b * BANK : (b + 1) * BANK],
                        start=(g == 0),
                        stop=(g == PASSES - 1),
                    )
                heads = acc[:].rearrange("p (h f i e) -> p h f i e", h=BANK_HEADS, f=2, e=2)
                result = results.tile([P, BANK], F32)
                res = result[:].rearrange("p (h f i e) -> p h f i e", h=BANK_HEADS, f=2, e=2)
                from_odd = work.tile([P, BANK_HEADS, PAIRS, 2], F32)
                nc.vector.tensor_tensor(
                    out=res[:, :, 1, :, :],
                    in0=heads[:, :, 1, :, 0:1].to_broadcast([P, BANK_HEADS, PAIRS, 2]),
                    in1=even_table,
                    op=ALU.mult,
                )
                nc.vector.tensor_tensor(
                    out=from_odd[:],
                    in0=heads[:, :, 1, :, 1:2].to_broadcast([P, BANK_HEADS, PAIRS, 2]),
                    in1=odd_table,
                    op=ALU.mult,
                )
                nc.gpsimd.tensor_tensor(
                    out=res[:, :, 1, :, :], in0=res[:, :, 1, :, :], in1=from_odd[:], op=ALU.add
                )
                nc.scalar.copy(out=res[:, :, 0, :, :], in_=heads[:, :, 0, :, :])
                nc.sync.dma_start(
                    out=out_rows[t * P : (t + 1) * P, c * BANK : (c + 1) * BANK], in_=result[:]
                )

        def project_last(t, s):
            half = t % (SEQ // P)
            shape = [P, BANK_HEADS, PAIRS, 2]
            even_table = by_even[:, half, :, :].unsqueeze(1).to_broadcast(shape)
            odd_table = by_odd[:, half, :, :].unsqueeze(1).to_broadcast(shape)
            banks = range(STRIPE_BANKS[s] - 2, STRIPE_BANKS[s])
            res = {b: results.tile([P, BANK_HEADS, 2, PAIRS, 2], F32, name="result") for b in banks}

            def half_head(acc, b, h, f):
                first = b * BANK + (2 * h + f) * 2 * PAIRS
                for g in range(PASSES):
                    nc.tensor.matmul_mx(
                        out=acc.rearrange("p i e -> p (i e)"),
                        lhsT=x_codes[t][:, g * P : (g + 1) * P].bitcast(FP8X4),
                        lhsT_scale=x_scales[t][:, g * P : (g + 1) * P],
                        rhs=words_of(s, g)[:, 2 * first : 2 * (first + 2 * PAIRS)].bitcast(FP4X4),
                        rhs_scale=w_scales[s][:, g, first : first + 2 * PAIRS],
                        start=(g == 0),
                        stop=(g == PASSES - 1),
                    )

            def store(b, heads, f):
                c = sum(STRIPE_BANKS[:s]) + b
                out_heads = out_rows[t * P : (t + 1) * P, c * BANK : (c + 1) * BANK].rearrange(
                    "p (h f i e) -> p h f i e", h=BANK_HEADS, f=2, e=2
                )
                nc.sync.dma_start(out=out_heads[:, heads, f, :, :], in_=res[b][:, heads, f, :, :])

            for b in banks:
                acc = psum.tile(shape, F32, name="bank")
                for h in range(BANK_HEADS):
                    half_head(acc[:, h, :, :], b, h, 1)
                rotated = res[b][:, :, 1, :, :]
                from_odd = work.tile(shape, F32)
                nc.vector.tensor_tensor(
                    out=rotated,
                    in0=acc[:, :, :, 0:1].to_broadcast(shape),
                    in1=even_table,
                    op=ALU.mult,
                )
                nc.vector.tensor_tensor(
                    out=from_odd[:],
                    in0=acc[:, :, :, 1:2].to_broadcast(shape),
                    in1=odd_table,
                    op=ALU.mult,
                )
                adder = nc.gpsimd if b == banks[0] else nc.vector
                adder.tensor_tensor(out=rotated, in0=rotated, in1=from_odd[:], op=ALU.add)
                store(b, slice(0, BANK_HEADS), 1)

            b = banks[0]
            acc = psum.tile(shape, F32, name="bank")
            for h in range(BANK_HEADS):
                half_head(acc[:, h, :, :], b, h, 0)
            nc.scalar.copy(out=res[b][:, :, 0, :, :], in_=acc[:])
            store(b, slice(0, BANK_HEADS), 0)

            b = banks[1]
            for h, copy in enumerate((nc.scalar.copy, nc.vector.tensor_copy)):
                acc = psum.tile([P, PAIRS, 2], F32, name="bank")
                half_head(acc[:], b, h, 0)
                copy(out=res[b][:, h, 0, :, :], in_=acc[:])
                store(b, slice(h, h + 1), 0)

        zero_words = keep.tile([P, BANK // 2], F32)
        nc.gpsimd.memset(zero_words[:], 0.0)
        zeros = zero_words[:].bitcast(BF16)
        idle_sums = psum.tile([P, BANK], F32, name="bank")

        def keep_warm(count):
            for i in range(count):
                nc.tensor.matmul(idle_sums[:], lhsT=zeros[:, 0:P], rhs=zeros, start=True, stop=True)

        keep_warm(4)

        for t in range(TOKEN_TILES):
            load_x(t)
        identity = keep.tile([P, P], F32)
        make_identity(nc, identity[:])

        warm = keep.tile([P, 1], F32)
        nc.vector.memset(warm[:], 0.0)
        nc.scalar.activation(out=warm[:], in_=warm[:], func=ACT.Sin)

        zero_scales(0)
        load_weight_stripe(0)
        reduced = reduce_angles(
            nc, keep, [lambda: zero_scales(1), lambda: zero_scales(2), lambda: None]
        )
        load_weight_stripe(1)
        load_weight_stripe(2)

        for t in range(TOKEN_TILES):
            quantise_x(t)
            if t == 1:
                zero_scales(3)
                load_weight_stripe(3)
            keep_warm(1 if t + 1 < TOKEN_TILES else 3)
        by_even, by_odd = build_rope_tables(nc, keep, *reduced)

        for s in range(STRIPES):
            for t in range(TOKEN_TILES):
                if (s, t) == (STRIPES - 1, TOKEN_TILES - 1):
                    project(t, s, range(STRIPE_BANKS[s] - 2))
                    project_last(t, s)
                else:
                    project(t, s, range(STRIPE_BANKS[s]))
